import numpy as np
import ml_dtypes


def mxq(x, axis, fmt="e4m3"):
    dtype, down = {"e4m3": (ml_dtypes.float8_e4m3fn, 7), "e5m2": (ml_dtypes.float8_e5m2, 14)}[fmt]
    v = np.moveaxis(np.asarray(x, np.float32).astype(ml_dtypes.bfloat16).astype(np.float64), axis, -1)
    blocks = v.reshape(v.shape[:-1] + (-1, 32))
    amax = np.abs(blocks).max(-1, keepdims=True)
    byte = np.maximum(np.where(amax > 0, np.frexp(amax)[1] - 1 + 127, 0) - down, 1)
    scale = np.exp2(byte - 127.0)
    codes = (blocks / scale).astype(np.float32).astype(dtype).astype(np.float64)
    return np.moveaxis((codes * scale).reshape(v.shape), -1, axis)


WIDE = False


def mx_kscale(k):
    if not WIDE:
        return np.ones(k)
    levels = np.array([20, -20, 10, -10, 0])
    a = np.random.permutation(np.resize(levels, k // 512 * 4)).reshape(k // 512, 4)
    idx = np.arange(k)
    return np.exp2(a[idx // 512, idx % 128 // 32])


BF16 = ml_dtypes.bfloat16


def bf(x):
    return np.asarray(x, np.float32).astype(BF16)


def f64(x):
    return np.asarray(x).astype(np.float64)


B, STACK, TUBE, CH, IMG, PATCH, EMBED = 16, 16, 4, 1, 128, 16, 1024
GH = IMG // PATCH
GW = IMG // PATCH
GD = STACK // TUBE
N = GD * GH * GW
K = TUBE * CH * PATCH * PATCH


def _sincos_1d(dim, pos):
    omega = 1.0 / (10000.0 ** (np.arange(dim // 2, dtype=np.float64) / (dim / 2.0)))
    out = pos[:, None].astype(np.float64) * omega[None, :]
    return np.concatenate([np.sin(out), np.cos(out)], axis=1)


def get_3d_sincos_pos_embed(grid_h, grid_w, grid_depth, embed_dim):
    dim_t = embed_dim // 4
    dim_s = embed_dim - dim_t
    emb_t = _sincos_1d(dim_t, np.arange(grid_depth))
    emb_h = _sincos_1d(dim_s // 2, np.arange(grid_h))
    emb_w = _sincos_1d(dim_s - dim_s // 2, np.arange(grid_w))
    emb_hw = np.concatenate([np.repeat(emb_h, grid_w, axis=0), np.tile(emb_w, (grid_h, 1))], axis=1)
    ns = grid_h * grid_w
    return np.concatenate([np.repeat(emb_t, ns, axis=0), np.tile(emb_hw, (grid_depth, 1))], axis=1)


def setup_inputs():
    u = mx_kscale(EMBED)
    video = np.random.standard_normal((B, STACK, CH, IMG, IMG))
    W = np.random.standard_normal((EMBED, K)) / np.sqrt(K) / u[:, None]
    b = np.random.standard_normal(EMBED) * 0.3
    pos_embed = get_3d_sincos_pos_embed(GH, GW, GD, EMBED)[None]
    g = np.random.standard_normal((B, N, EMBED)) * np.exp2(np.random.randint(-12, 1, (B, N, 1))) * 4.0 * u[None, None, :]
    return {"video": bf(video), "W": bf(W), "b": bf(b), "pos_embed": bf(pos_embed), "grad_out": bf(g)}


def reference(video, W, b, pos_embed, grad_out):
    g = f64(grad_out)
    gt = mxq(g, 2, "e5m2") @ mxq(f64(W), 0, "e4m3")
    nb = gt.shape[0]
    gt = gt.reshape(nb, GD, GH, GW, TUBE, CH, PATCH, PATCH)
    gt = gt.transpose(0, 1, 4, 5, 2, 6, 3, 7)
    return gt.reshape(nb, STACK, CH, IMG, IMG)

@@ -1,0 +1,178 @@
+from contextlib import ExitStack
+
+import concourse.mybir as mybir
+from concourse.masks import make_identity
+
+F32 = mybir.dt.float32
+BF16 = mybir.dt.bfloat16
+U32 = mybir.dt.uint32
+U8 = mybir.dt.uint8
+E5M2_X4 = mybir.dt.float8_e5m2_x4
+E4M3_X4 = mybir.dt.float8_e4m3fn_x4
+
+P = 128
+PACK = 4
+K_PASS = P * PACK
+PAIR = 2
+WORD_PLANES = PACK // PAIR
+
+BATCH = 16
+EMBED = 1024
+FEATURES = 1024
+PASSES = EMBED // K_PASS
+TUBES = 4
+TUBE_FRAMES = 4
+GRID = 8
+PATCH = 16
+GROUP_BATCHES = P // (TUBES * GRID)
+GROUPS = BATCH // GROUP_BATCHES
+N_TILE = 512
+HALVES = FEATURES // N_TILE
+HALF_FRAMES = TUBE_FRAMES // HALVES
+BLOCK = 4
+PARTS = GRID // BLOCK
+FIRST_LOAD_TILES = 2
+PSUM_BANKS = 8
+RESULT_BUFS = 5
+
+FLOPS = 2 * BATCH * TUBES * GRID * GRID * EMBED * FEATURES
+BYTES = 2 * BATCH * TUBES * GRID * GRID * EMBED + 2 * EMBED * FEATURES + 4 * BATCH * TUBES * GRID * GRID * FEATURES
+
+
+def tile_tubeletembedding_t_kernel(tc, video, W, b, pos_embed, grad_out, out):
+    nc = tc.nc
+    with ExitStack() as ctx:
+        const = ctx.enter_context(tc.tile_pool(name="const", bufs=1))
+        loaded = ctx.enter_context(tc.tile_pool(name="loaded", bufs=1))
+        weights = ctx.enter_context(tc.tile_pool(name="weights", bufs=1))
+        stage = ctx.enter_context(tc.tile_pool(name="stage", bufs=2))
+        operands = ctx.enter_context(tc.tile_pool(name="operands", bufs=2 * PARTS))
+        results = ctx.enter_context(tc.tile_pool(name="results", bufs=RESULT_BUFS))
+        psum = ctx.enter_context(tc.psum_pool(name="psum", bufs=PSUM_BANKS))
+        ctx.enter_context(tc.manual_schedule())
+
+        ident = const.tile([P, P], F32)
+        make_identity(nc, ident[:])
+
+        def load_w_half(half):
+            raw = loaded.tile([P, PASSES, PACK, N_TILE], BF16, name="w_raw_%d" % half)
+            for c in range(PASSES):
+                for u in range(WORD_PLANES):
+                    first = K_PASS * c + PAIR * P * u
+                    nc.sync.dma_start(
+                        out=raw[:, c, PAIR * u : PAIR * (u + 1), :],
+                        in_=W[first : first + PAIR * P, half * N_TILE : (half + 1) * N_TILE].rearrange(
+                            "(p r) k -> p r k", r=PAIR
+                        ),
+                    )
+            return raw
+
+        token_tile = {}
+
+        def load_token_tiles(group, first_j, count):
+            rows = grad_out[group * GROUP_BATCHES : (group + 1) * GROUP_BATCHES].rearrange(
+                "b (m j) e -> (b m) j e", j=GRID
+            )
+            chunk = loaded.tile([P, count, EMBED], BF16, name="g_raw_%d_%d" % (group, first_j))
+            nc.sync.dma_start(out=chunk[:], in_=rows[:, first_j : first_j + count, :])
+            for n in range(count):
+                token_tile[(group, first_j + n)] = chunk[:, n, :]
+
+        w_raw = {}
+        w_raw[0] = load_w_half(0)
+        for first_j in range(0, GRID, FIRST_LOAD_TILES):
+            load_token_tiles(0, first_j, FIRST_LOAD_TILES)
+        w_raw[1] = load_w_half(1)
+        for group in range(1, GROUPS):
+            for part in range(PARTS):
+                load_token_tiles(group, part * BLOCK, BLOCK)
+
+        w_codes = {}
+        w_scales = {}
+
+        def prepare_w_half(half):
+            grouped = weights.tile([P, PASSES, N_TILE, PACK], BF16, name="w_grouped", align_bytes=64)
+            codes = weights.tile([P, PASSES, N_TILE], U32, name="w_codes_%d" % half, align_bytes=64)
+            scales = weights.tile([P, PASSES, N_TILE], U8, name="w_scales_%d" % half, align_bytes=64)
+            for c in range(PASSES):
+                nc.vector.tensor_copy(
+                    out=grouped[:, c].rearrange("p (q n) t -> p q t n", n=4),
+                    in_=w_raw[half][:, c].rearrange("p t (q n) -> p q t n", n=4),
+                )
+            for c in range(PASSES):
+                nc.vector.quantize_mx(
+                    out=codes[:, c, :].bitcast(E4M3_X4),
+                    scales=scales[:, c, :],
+                    in_=grouped[:, c].rearrange("p k t -> p (k t)"),
+                )
+            w_codes[half] = codes
+            w_scales[half] = scales
+
+        def transpose_block(group, part, copy_out):
+            grouped = stage.tile([P, BLOCK, PASSES, P, WORD_PLANES], F32, name="g_grouped", align_bytes=64)
+            for n in range(BLOCK):
+                words = token_tile[(group, part * BLOCK + n)].bitcast(F32)
+                turned = psum.tile([P, PASSES * WORD_PLANES, P], F32, tag="bank")
+                for plane in range(PASSES * WORD_PLANES):
+                    nc.tensor.transpose(turned[:, plane, :], words[:, plane * P : (plane + 1) * P], ident[:])
+                copy_out(out=grouped[:, n], in_=turned[:].rearrange("p (c u) m -> p c m u", u=WORD_PLANES))
+            return grouped
+
+        g_codes = {}
+        g_scales = {}
+
+        def quantise_block(group, part, grouped):
+            codes = operands.tile([P, BLOCK, PASSES, P], U32, name="g_codes", align_bytes=64)
+            scales = operands.tile([P, BLOCK, PASSES, P], U8, name="g_scales", align_bytes=64)
+            nc.vector.quantize_mx(
+                out=codes[:].rearrange("p n c m -> p (n c m)").bitcast(E5M2_X4),
+                scales=scales[:].rearrange("p n c m -> p (n c m)"),
+                in_=grouped[:].rearrange("p n c m u -> p (n c m u)").bitcast(BF16),
+            )
+            g_codes[(group, part)] = codes
+            g_scales[(group, part)] = scales
+
+        def multiply_block(group, half, part, result):
+            for n in range(BLOCK):
+                product = psum.tile([P, N_TILE], F32, tag="bank")
+                for c in range(PASSES):
+                    nc.tensor.matmul_mx(
+                        out=product[:],
+                        lhsT=g_codes[(group, part)][:, n, c, :].bitcast(E5M2_X4),
+                        lhsT_scale=g_scales[(group, part)][:, n, c, :],
+                        rhs=w_codes[half][:, c, :].bitcast(E4M3_X4),
+                        rhs_scale=w_scales[half][:, c, :],
+                        start=(c == 0),
+                        stop=(c == PASSES - 1),
+                    )
+                nc.scalar.copy(
+                    out=result[:, :, :, part * BLOCK + n, :],
+                    in_=product[:].rearrange("p (s y x) -> p s y x", s=HALF_FRAMES, y=PATCH),
+                )
+
+        def store_result(group, half, result):
+            frames = out[group * GROUP_BATCHES : (group + 1) * GROUP_BATCHES].rearrange(
+                "b (d s) c (i y) w -> s (b d) i (c y w)", s=TUBE_FRAMES, y=PATCH
+            )
+            for s in range(HALF_FRAMES):
+                nc.sync.dma_start(
+                    out=frames[half * HALF_FRAMES + s],
+                    in_=result[:, s].rearrange("p y j x -> p (y j x)"),
+                )
+
+        prepare_w_half(0)
+        for part in range(PARTS):
+            quantise_block(0, part, transpose_block(0, part, nc.scalar.copy))
+        prepare_w_half(1)
+
+        for group in range(GROUPS):
+            for half in range(HALVES):
+                result = results.tile([P, HALF_FRAMES, PATCH, GRID, PATCH], F32, name="result")
+                for part in range(PARTS):
+                    ahead = half == HALVES - 1 and group + 1 < GROUPS
+                    if ahead:
+                        grouped = transpose_block(group + 1, part, nc.vector.tensor_copy)
+                    multiply_block(group, half, part, result)
+                    if ahead:
+                        quantise_block(group + 1, part, grouped)
+                store_result(group, half, result)

@@ -132,7 +132,7 @@ def tile_tubeletembedding_t_kernel(tc, video, W, b, pos_embed, grad_out, out):
             g_codes[(group, part)] = codes
             g_scales[(group, part)] = scales
 
-        def multiply_block(group, half, part, result):
+        def multiply_block(group, half, part, result, vector_is_free):
             for n in range(BLOCK):
                 product = psum.tile([P, N_TILE], F32, tag="bank")
                 for c in range(PASSES):
@@ -145,7 +145,8 @@ def tile_tubeletembedding_t_kernel(tc, video, W, b, pos_embed, grad_out, out):
                         start=(c == 0),
                         stop=(c == PASSES - 1),
                     )
-                nc.scalar.copy(
+                copy_out = nc.vector.tensor_copy if vector_is_free and n % 2 == 1 else nc.scalar.copy
+                copy_out(
                     out=result[:, :, :, part * BLOCK + n, :],
                     in_=product[:].rearrange("p (s y x) -> p s y x", s=HALF_FRAMES, y=PATCH),
                 )
@@ -172,7 +173,7 @@ def tile_tubeletembedding_t_kernel(tc, video, W, b, pos_embed, grad_out, out):
                     ahead = half == HALVES - 1 and group + 1 < GROUPS
                     if ahead:
                         grouped = transpose_block(group + 1, part, nc.vector.tensor_copy)
-                    multiply_block(group, half, part, result)
+                    multiply_block(group, half, part, result, not ahead)
                     if ahead:
                         quantise_block(group + 1, part, grouped)
                 store_result(group, half, result)

@@ -48,8 +48,15 @@ def tile_tubeletembedding_t_kernel(tc, video, W, b, pos_embed, grad_out, out):
         stage = ctx.enter_context(tc.tile_pool(name="stage", bufs=2))
         operands = ctx.enter_context(tc.tile_pool(name="operands", bufs=2 * PARTS))
         results = ctx.enter_context(tc.tile_pool(name="results", bufs=RESULT_BUFS))
-        psum = ctx.enter_context(tc.psum_pool(name="psum", bufs=PSUM_BANKS))
+        psum = ctx.enter_context(tc.psum_pool(name="psum", bufs=1))
         ctx.enter_context(tc.manual_schedule())
+
+        banks_taken = [0]
+
+        def next_bank(shape):
+            bank = psum.tile(shape, F32, name="bank", tag="bank_%d" % (banks_taken[0] % PSUM_BANKS))
+            banks_taken[0] += 1
+            return bank
 
         ident = const.tile([P, P], F32)
         make_identity(nc, ident[:])
@@ -112,7 +119,7 @@ def tile_tubeletembedding_t_kernel(tc, video, W, b, pos_embed, grad_out, out):
             grouped = stage.tile([P, BLOCK, PASSES, P, WORD_PLANES], F32, name="g_grouped", align_bytes=64)
             for n in range(BLOCK):
                 words = token_tile[(group, part * BLOCK + n)].bitcast(F32)
-                turned = psum.tile([P, PASSES * WORD_PLANES, P], F32, tag="bank")
+                turned = next_bank([P, PASSES * WORD_PLANES, P])
                 for plane in range(PASSES * WORD_PLANES):
                     nc.tensor.transpose(turned[:, plane, :], words[:, plane * P : (plane + 1) * P], ident[:])
                 copy_out(out=grouped[:, n], in_=turned[:].rearrange("p (c u) m -> p c m u", u=WORD_PLANES))
@@ -132,9 +139,9 @@ def tile_tubeletembedding_t_kernel(tc, video, W, b, pos_embed, grad_out, out):
             g_codes[(group, part)] = codes
             g_scales[(group, part)] = scales
 
-        def multiply_block(group, half, part, result, vector_is_free):
+        def multiply_block(group, half, part, result):
             for n in range(BLOCK):
-                product = psum.tile([P, N_TILE], F32, tag="bank")
+                product = next_bank([P, N_TILE])
                 for c in range(PASSES):
                     nc.tensor.matmul_mx(
                         out=product[:],
@@ -145,8 +152,7 @@ def tile_tubeletembedding_t_kernel(tc, video, W, b, pos_embed, grad_out, out):
                         start=(c == 0),
                         stop=(c == PASSES - 1),
                     )
-                copy_out = nc.vector.tensor_copy if vector_is_free and n % 2 == 1 else nc.scalar.copy
-                copy_out(
+                nc.scalar.copy(
                     out=result[:, :, :, part * BLOCK + n, :],
                     in_=product[:].rearrange("p (s y x) -> p s y x", s=HALF_FRAMES, y=PATCH),
                 )
@@ -173,7 +179,7 @@ def tile_tubeletembedding_t_kernel(tc, video, W, b, pos_embed, grad_out, out):
                     ahead = half == HALVES - 1 and group + 1 < GROUPS
                     if ahead:
                         grouped = transpose_block(group + 1, part, nc.vector.tensor_copy)
-                    multiply_block(group, half, part, result, not ahead)
+                    multiply_block(group, half, part, result)
                     if ahead:
                         quantise_block(group + 1, part, grouped)
                 store_result(group, half, result)

@@ -162,7 +162,7 @@ def tile_tubeletembedding_t_kernel(tc, video, W, b, pos_embed, grad_out, out):
                 "b (d s) c (i y) w -> s (b d) i (c y w)", s=TUBE_FRAMES, y=PATCH
             )
             for s in range(HALF_FRAMES):
-                nc.sync.dma_start(
+                nc.scalar.dma_start(
                     out=frames[half * HALF_FRAMES + s],
                     in_=result[:, s].rearrange("p y j x -> p (y j x)"),
                 )

from contextlib import ExitStack

import concourse.mybir as mybir
from concourse.masks import make_identity

F32 = mybir.dt.float32
BF16 = mybir.dt.bfloat16
U32 = mybir.dt.uint32
U8 = mybir.dt.uint8
E5M2_X4 = mybir.dt.float8_e5m2_x4
E4M3_X4 = mybir.dt.float8_e4m3fn_x4

P = 128
PACK = 4
K_PASS = P * PACK
PAIR = 2
WORD_PLANES = PACK // PAIR

BATCH = 16
EMBED = 1024
FEATURES = 1024
PASSES = EMBED // K_PASS
TUBES = 4
TUBE_FRAMES = 4
GRID = 8
PATCH = 16
GROUP_BATCHES = P // (TUBES * GRID)
GROUPS = BATCH // GROUP_BATCHES
N_TILE = 512
HALVES = FEATURES // N_TILE
HALF_FRAMES = TUBE_FRAMES // HALVES
BLOCK = 4
PARTS = GRID // BLOCK
FIRST_LOAD_TILES = 2
PSUM_BANKS = 8
RESULT_BUFS = 5

FLOPS = 2 * BATCH * TUBES * GRID * GRID * EMBED * FEATURES
BYTES = 2 * BATCH * TUBES * GRID * GRID * EMBED + 2 * EMBED * FEATURES + 4 * BATCH * TUBES * GRID * GRID * FEATURES


def tile_tubeletembedding_t_kernel(tc, video, W, b, pos_embed, grad_out, out):
    nc = tc.nc
    with ExitStack() as ctx:
        const = ctx.enter_context(tc.tile_pool(name="const", bufs=1))
        loaded = ctx.enter_context(tc.tile_pool(name="loaded", bufs=1))
        weights = ctx.enter_context(tc.tile_pool(name="weights", bufs=1))
        stage = ctx.enter_context(tc.tile_pool(name="stage", bufs=2))
        operands = ctx.enter_context(tc.tile_pool(name="operands", bufs=2 * PARTS))
        results = ctx.enter_context(tc.tile_pool(name="results", bufs=RESULT_BUFS))
        psum = ctx.enter_context(tc.psum_pool(name="psum", bufs=1))
        ctx.enter_context(tc.manual_schedule())

        banks_taken = [0]

        def next_bank(shape):
            bank = psum.tile(shape, F32, name="bank", tag="bank_%d" % (banks_taken[0] % PSUM_BANKS))
            banks_taken[0] += 1
            return bank

        ident = const.tile([P, P], F32)
        make_identity(nc, ident[:])

        def load_w_half(half):
            raw = loaded.tile([P, PASSES, PACK, N_TILE], BF16, name="w_raw_%d" % half)
            for c in range(PASSES):
                for u in range(WORD_PLANES):
                    first = K_PASS * c + PAIR * P * u
                    nc.sync.dma_start(
                        out=raw[:, c, PAIR * u : PAIR * (u + 1), :],
                        in_=W[first : first + PAIR * P, half * N_TILE : (half + 1) * N_TILE].rearrange(
                            "(p r) k -> p r k", r=PAIR
                        ),
                    )
            return raw

        token_tile = {}

        def load_token_tiles(group, first_j, count):
            rows = grad_out[group * GROUP_BATCHES : (group + 1) * GROUP_BATCHES].rearrange(
                "b (m j) e -> (b m) j e", j=GRID
            )
            chunk = loaded.tile([P, count, EMBED], BF16, name="g_raw_%d_%d" % (group, first_j))
            nc.sync.dma_start(out=chunk[:], in_=rows[:, first_j : first_j + count, :])
            for n in range(count):
                token_tile[(group, first_j + n)] = chunk[:, n, :]

        w_raw = {}
        w_raw[0] = load_w_half(0)
        for first_j in range(0, GRID, FIRST_LOAD_TILES):
            load_token_tiles(0, first_j, FIRST_LOAD_TILES)
        w_raw[1] = load_w_half(1)
        for group in range(1, GROUPS):
            for part in range(PARTS):
                load_token_tiles(group, part * BLOCK, BLOCK)

        w_codes = {}
        w_scales = {}

        def prepare_w_half(half):
            grouped = weights.tile([P, PASSES, N_TILE, PACK], BF16, name="w_grouped", align_bytes=64)
            codes = weights.tile([P, PASSES, N_TILE], U32, name="w_codes_%d" % half, align_bytes=64)
            scales = weights.tile([P, PASSES, N_TILE], U8, name="w_scales_%d" % half, align_bytes=64)
            for c in range(PASSES):
                nc.vector.tensor_copy(
                    out=grouped[:, c].rearrange("p (q n) t -> p q t n", n=4),
                    in_=w_raw[half][:, c].rearrange("p t (q n) -> p q t n", n=4),
                )
            for c in range(PASSES):
                nc.vector.quantize_mx(
                    out=codes[:, c, :].bitcast(E4M3_X4),
                    scales=scales[:, c, :],
                    in_=grouped[:, c].rearrange("p k t -> p (k t)"),
                )
            w_codes[half] = codes
            w_scales[half] = scales

        def transpose_block(group, part, copy_out):
            grouped = stage.tile([P, BLOCK, PASSES, P, WORD_PLANES], F32, name="g_grouped", align_bytes=64)
            for n in range(BLOCK):
                words = token_tile[(group, part * BLOCK + n)].bitcast(F32)
                turned = next_bank([P, PASSES * WORD_PLANES, P])
                for plane in range(PASSES * WORD_PLANES):
                    nc.tensor.transpose(turned[:, plane, :], words[:, plane * P : (plane + 1) * P], ident[:])
                copy_out(out=grouped[:, n], in_=turned[:].rearrange("p (c u) m -> p c m u", u=WORD_PLANES))
            return grouped

        g_codes = {}
        g_scales = {}

        def quantise_block(group, part, grouped):
            codes = operands.tile([P, BLOCK, PASSES, P], U32, name="g_codes", align_bytes=64)
            scales = operands.tile([P, BLOCK, PASSES, P], U8, name="g_scales", align_bytes=64)
            nc.vector.quantize_mx(
                out=codes[:].rearrange("p n c m -> p (n c m)").bitcast(E5M2_X4),
                scales=scales[:].rearrange("p n c m -> p (n c m)"),
                in_=grouped[:].rearrange("p n c m u -> p (n c m u)").bitcast(BF16),
            )
            g_codes[(group, part)] = codes
            g_scales[(group, part)] = scales

        def multiply_block(group, half, part, result):
            for n in range(BLOCK):
                product = next_bank([P, N_TILE])
                for c in range(PASSES):
                    nc.tensor.matmul_mx(
                        out=product[:],
                        lhsT=g_codes[(group, part)][:, n, c, :].bitcast(E5M2_X4),
                        lhsT_scale=g_scales[(group, part)][:, n, c, :],
                        rhs=w_codes[half][:, c, :].bitcast(E4M3_X4),
                        rhs_scale=w_scales[half][:, c, :],
                        start=(c == 0),
                        stop=(c == PASSES - 1),
                    )
                nc.scalar.copy(
                    out=result[:, :, :, part * BLOCK + n, :],
                    in_=product[:].rearrange("p (s y x) -> p s y x", s=HALF_FRAMES, y=PATCH),
                )

        def store_result(group, half, result):
            frames = out[group * GROUP_BATCHES : (group + 1) * GROUP_BATCHES].rearrange(
                "b (d s) c (i y) w -> s (b d) i (c y w)", s=TUBE_FRAMES, y=PATCH
            )
            for s in range(HALF_FRAMES):
                nc.scalar.dma_start(
                    out=frames[half * HALF_FRAMES + s],
                    in_=result[:, s].rearrange("p y j x -> p (y j x)"),
                )

        prepare_w_half(0)
        for part in range(PARTS):
            quantise_block(0, part, transpose_block(0, part, nc.scalar.copy))
        prepare_w_half(1)

        for group in range(GROUPS):
            for half in range(HALVES):
                result = results.tile([P, HALF_FRAMES, PATCH, GRID, PATCH], F32, name="result")
                for part in range(PARTS):
                    ahead = half == HALVES - 1 and group + 1 < GROUPS
                    if ahead:
                        grouped = transpose_block(group + 1, part, nc.vector.tensor_copy)
                    multiply_block(group, half, part, result)
                    if ahead:
                        quantise_block(group + 1, part, grouped)
                store_result(group, half, result)
